import numpy as np
import ml_dtypes


def mxq(x, axis, fmt="e4m3"):
    dtype, down = {"e4m3": (ml_dtypes.float8_e4m3fn, 7), "e5m2": (ml_dtypes.float8_e5m2, 14)}[fmt]
    v = np.moveaxis(np.asarray(x, np.float32).astype(ml_dtypes.bfloat16).astype(np.float64), axis, -1)
    blocks = v.reshape(v.shape[:-1] + (-1, 32))
    amax = np.abs(blocks).max(-1, keepdims=True)
    byte = np.maximum(np.where(amax > 0, np.frexp(amax)[1] - 1 + 127, 0) - down, 1)
    scale = np.exp2(byte - 127.0)
    codes = (blocks / scale).astype(np.float32).astype(dtype).astype(np.float64)
    return np.moveaxis((codes * scale).reshape(v.shape), -1, axis)


WIDE = False


def mx_kscale(k):
    if not WIDE:
        return np.ones(k)
    levels = np.array([10, -10, 5, -5, 0])
    if k % 512:
        return np.exp2(np.random.permutation(np.resize(levels, k // 32))).repeat(32)
    a = np.empty((k // 512, 16))
    for p in range(k // 512):
        a[p, :8] = np.random.permutation(np.resize(levels, 8))
        for g in range(8):
            far = levels[np.abs(levels - a[p, g]) >= 10]
            a[p, g + 8] = far[np.random.randint(len(far))]
    return np.exp2(a.ravel()).repeat(32)


BF16 = ml_dtypes.bfloat16


def bf(x):
    return np.asarray(x, np.float32).astype(BF16)


def f64(x):
    return np.asarray(x).astype(np.float64)


E2M1 = np.array([0.0, 0.5, 1.0, 1.5, 2.0, 3.0, 4.0, 6.0, -0.0, -0.5, -1.0, -1.5, -2.0, -3.0, -4.0, -6.0])


def pack_weight(w, fmt):
    k, n = w.shape
    w = f64(bf(w)).reshape(k // 32, 32, n)
    amax = np.abs(w).max(1)
    if fmt == "e4m3":
        byte = np.frexp(amax)[1] - 1 + 127 - 7
    else:
        mant, ex = np.frexp(amax / 6.0)
        byte = np.where(mant > 0.5, ex, ex - 1) + 127
    byte = np.clip(np.where(amax > 0, byte, 1), 1, 254)
    scaled = (w * np.exp2(127.0 - byte)[:, None, :]).reshape(k, n).astype(np.float32)
    by_word = np.ascontiguousarray(scaled.reshape(k // 512, 128, 4, n).transpose(0, 1, 3, 2))
    if fmt == "e4m3":
        words = by_word.astype(ml_dtypes.float8_e4m3fn).view(np.uint8)
    else:
        c = by_word.astype(ml_dtypes.float4_e2m1fn).view(np.uint8) & 0xF
        words = c[..., 0::2] | (c[..., 1::2] << 4)
    return np.ascontiguousarray(words), np.ascontiguousarray(byte.astype(np.uint8).reshape(k // 512, 16, n))


def unpack_weight(words, scales, fmt):
    g, p, n, _ = words.shape
    if fmt == "e4m3":
        vals = np.ascontiguousarray(words).view(ml_dtypes.float8_e4m3fn).astype(np.float64)
    else:
        nib = np.empty((g, p, n, 4), np.uint8)
        nib[..., 0::2] = words & 0xF
        nib[..., 1::2] = words >> 4
        vals = E2M1[nib]
    vals = vals * np.repeat(np.exp2(scales.astype(np.float64) - 127.0), 8, axis=1)[..., None]
    return vals.transpose(0, 1, 3, 2).reshape(g * 512, n)


N, DIN, H1, H2, C, NC, G = 1024, 512, 512, 256, 128, 512, 8


def draw0():
    s, t = mx_kscale(N), mx_kscale(DIN)
    F_ = bf(np.random.uniform(size=(N, N)) * 2.0 / np.sqrt(N) * s)
    X = bf(np.random.standard_normal((N, DIN)) / s[:, None] * t)
    words, scales = pack_weight(np.random.standard_normal((DIN, H1)) * 0.8 / np.sqrt(DIN) / t[:, None], "e4m3")
    return {"F_": F_,
            "X": X,
            "W1_words": words,
            "W1_scales": scales,
            "b1": bf(np.random.standard_normal(H1) * 0.3)}


def core(F_, X, W1_words, W1_scales, b1):
    agg = mxq(f64(F_), 1, "e4m3") @ mxq(f64(X), 0, "e4m3")
    return np.tanh((mxq(agg, 1, "e4m3") @ unpack_weight(W1_words, W1_scales, "e4m3")) + f64(b1))


def e4m3fn_bytes(y):
    return np.clip(np.asarray(y, np.float64), -448.0, 448.0).astype(np.float32).astype(ml_dtypes.float8_e4m3fn).view(np.uint8)


def e4m3fn_values(b):
    return np.asarray(b, np.uint8).view(ml_dtypes.float8_e4m3fn).astype(np.float64)


def setup_inputs():
    d = draw0()
    x0 = np.asarray(d['F_']).astype(np.float64)
    s = (np.max(np.abs(x0), axis=(0,), keepdims=True) / 448.0).astype(np.float32)
    out = {}
    for k, v in d.items():
        if k == 'F_':
            out['F__bytes'] = e4m3fn_bytes(x0 / s.astype(np.float64))
            out['F__scale'] = s
        else:
            out[k] = v
    return out


def reference(F__bytes, F__scale, X, W1_words, W1_scales, b1):
    return core(e4m3fn_values(F__bytes) * F__scale.astype(np.float64), X, W1_words, W1_scales, b1)

@@ -1,0 +1,182 @@
+from contextlib import ExitStack
+
+import concourse.mybir as mybir
+from concourse.masks import make_identity
+
+F32 = mybir.dt.float32
+BF16 = mybir.dt.bfloat16
+U32 = mybir.dt.uint32
+I32 = mybir.dt.int32
+U8 = mybir.dt.uint8
+FP8 = mybir.dt.float8_e4m3fn
+FP8X4 = mybir.dt.float8_e4m3fn_x4
+MULT = mybir.AluOpType.mult
+ADD = mybir.AluOpType.add
+ACT = mybir.ActivationFunctionType
+
+P = 128
+NODES = 1024
+DIN = 512
+H = 512
+G = 2
+T = 4
+TILES = 8
+LAG = 3
+FLOPS = 2 * NODES * NODES * DIN + 2 * NODES * DIN * H
+
+
+def tile_controencodnet_pa_w8_kernel(tc, f_bytes, f_scale, x, w_words, w_scales, b1, out):
+    nc = tc.nc
+    with ExitStack() as ctx:
+        keep = ctx.enter_context(tc.tile_pool(name="keep", bufs=1))
+        ring = ctx.enter_context(tc.tile_pool(name="ring", bufs=4))
+        ps_t = ctx.enter_context(tc.psum_pool(name="ps_t", bufs=3))
+        ps_a = ctx.enter_context(tc.psum_pool(name="ps_a", bufs=2))
+        ps_o = ctx.enter_context(tc.psum_pool(name="ps_o", bufs=3))
+        ctx.enter_context(tc.manual_schedule())
+
+        bytes_src = f_bytes.rearrange("(p i) k -> p i k", i=TILES)
+        out_dst = out.rearrange("(p i) h -> p i h", i=TILES)
+        x_src = x.rearrange("(g p j) d -> g p j d", g=G, j=T)
+
+        loads = [(0, 1), (1, 2), (2, 4), (4, 6), (6, 8)]
+        fb = [keep.tile([P, (b - a) * NODES], U8, name="fb%d" % a, align_bytes=64) for a, b in loads]
+        where = {}
+        for q, (a, b) in enumerate(loads):
+            for i in range(a, b):
+                where[i] = (q, i - a)
+        fs = keep.tile([P, G, T], F32)
+        xr = [keep.tile([P, T, DIN], BF16, name="xr%d" % g, align_bytes=64) for g in range(G)]
+        xg = [keep.tile([P, T * P * T], BF16, name="xg%d" % g, align_bytes=64) for g in range(G)]
+        xc = [keep.tile([P, DIN], U32, name="xc%d" % g, align_bytes=64) for g in range(G)]
+        xs = [keep.tile([P, DIN], U8, name="xs%d" % g, align_bytes=64) for g in range(G)]
+        wc = keep.tile([P, H * T], U8, align_bytes=64)
+        ws = keep.tile([P, H], U8, align_bytes=64)
+        bias = keep.tile([P, H], BF16)
+        ident = keep.tile([P, P], F32)
+        warm = keep.tile([P, 1], F32)
+
+        def load_f(q):
+            a, b = loads[q]
+            nc.sync.dma_start(out=fb[q][:].rearrange("p (i k) -> p i k", i=b - a), in_=bytes_src[:, a:b, :])
+
+        load_f(0)
+        nc.sync.dma_start(out=fs[:], in_=f_scale.rearrange("o (g p t) -> p (o g) t", g=G, t=T))
+        nc.sync.dma_start(out=xr[0][:], in_=x_src[0])
+        load_f(1)
+        nc.sync.dma_start(out=xr[1][:], in_=x_src[1])
+        load_f(2)
+        nc.vector.memset(warm[:], 0.0)
+        nc.scalar.activation(out=warm[:], in_=warm[:], func=ACT.Tanh)
+        make_identity(nc, ident[:])
+        nc.gpsimd.memset(ws[:].bitcast(U32), 0)
+        load_f(3)
+        nc.sync.dma_start(out=wc[:], in_=w_words[0].rearrange("p n t -> p (n t)"))
+        for q in range(4):
+            nc.sync.dma_start(out=ws[32 * q : 32 * q + 4, :].bitcast(I32), in_=w_scales[0, 4 * q : 4 * q + 4, :].bitcast(I32))
+        load_f(4)
+        nc.sync.dma_start(out=bias[:], in_=b1.partition_broadcast(P))
+
+        wide, turned, fg, fc, fsc = {}, {}, {}, {}, {}
+        agg, ag, ac, asc, prod, summed, res = {}, {}, {}, {}, {}, {}, {}
+
+        def cast(i):
+            q, k = where[i]
+            wide[i] = ring.tile([P, NODES], BF16, name="wide", align_bytes=64)
+            nc.scalar.copy(out=wide[i][:], in_=fb[q][:, k * NODES : (k + 1) * NODES].bitcast(FP8))
+
+        def turn(i):
+            turned[i] = ps_t.tile([P, 2, G, P], F32, name="turned")
+            words = wide[i][:].bitcast(F32)
+            for g in range(G):
+                for u in range(2):
+                    nc.tensor.transpose(turned[i][:, u, g, :], words[:, 256 * g + u : 256 * (g + 1) : 2], ident[:])
+
+        def multiply(i):
+            fg[i] = ring.tile([P, G, P * T], BF16, name="fg", align_bytes=64)
+            nc.vector.tensor_tensor(
+                out=fg[i][:].rearrange("p g (n u e) -> p g n u e", u=2, e=2),
+                in0=turned[i][:].rearrange("p u g n -> p (u g n)").bitcast(BF16).rearrange("p (u g n e) -> p g n u e", u=2, g=G, e=2),
+                in1=fs[:].unsqueeze(2).to_broadcast([P, G, P, T]).rearrange("p g n (u e) -> p g n u e", u=2),
+                op=MULT,
+            )
+
+        def quantize_f(i):
+            fc[i] = ring.tile([P, G * P], U32, name="fc", align_bytes=64)
+            fsc[i] = ring.tile([P, G * P], U8, name="fsc", align_bytes=64)
+            nc.vector.quantize_mx(out=fc[i][:].bitcast(FP8X4), scales=fsc[i][:], in_=fg[i][:].rearrange("p g n -> p (g n)"))
+
+        def interleave_x(g, t0, t1, engine):
+            dst = xg[g][:].rearrange("p (t m j) -> p t m j", t=T, j=T)[:, t0:t1]
+            src = xr[g][:].rearrange("p j (m t) -> p t m j", t=T)[:, t0:t1]
+            if engine == "v":
+                nc.vector.tensor_copy(out=dst, in_=src)
+            elif engine == "s":
+                nc.scalar.copy(out=dst, in_=src)
+            else:
+                nc.gpsimd.tensor_scalar(out=dst, in0=src, scalar1=1.0, scalar2=0.0, op0=MULT, op1=ADD)
+
+        def quantize_x(g):
+            nc.vector.quantize_mx(out=xc[g][:].bitcast(FP8X4), scales=xs[g][:], in_=xg[g][:])
+
+        def mm1(i):
+            agg[i] = ps_a.tile([P, T, P], F32, name="agg")
+            for t in range(T):
+                cols = slice(P * t, P * (t + 1))
+                for g in range(G):
+                    rows = slice(P * g, P * (g + 1))
+                    nc.tensor.matmul_mx(out=agg[i][:, t, :], lhsT=xc[g][:, cols].bitcast(FP8X4), lhsT_scale=xs[g][:, cols],
+                                        rhs=fc[i][:, rows].bitcast(FP8X4), rhs_scale=fsc[i][:, rows], start=(g == 0), stop=(g == G - 1))
+
+        def evacuate(i):
+            ag[i] = ring.tile([P, P * T], BF16, name="ag", align_bytes=64)
+            nc.scalar.copy(out=ag[i][:].rearrange("p (n t) -> p n t", t=T), in_=agg[i][:].rearrange("p t n -> p n t"))
+
+        def quantize_a(i):
+            ac[i] = ring.tile([P, P], U32, name="ac", align_bytes=64)
+            asc[i] = ring.tile([P, P], U8, name="asc", align_bytes=64)
+            nc.vector.quantize_mx(out=ac[i][:].bitcast(FP8X4), scales=asc[i][:], in_=ag[i][:])
+
+        def mm2(i):
+            prod[i] = ps_o.tile([P, H], F32, name="prod")
+            nc.tensor.matmul_mx(out=prod[i][:], lhsT=ac[i][:].bitcast(FP8X4), lhsT_scale=asc[i][:], rhs=wc[:].bitcast(FP8X4), rhs_scale=ws[:], start=True, stop=True)
+
+        def add_bias(i):
+            summed[i] = ring.tile([P, H], F32, name="summed")
+            nc.vector.tensor_tensor(out=summed[i][:], in0=prod[i][:], in1=bias[:], op=ADD)
+
+        def finish(i):
+            res[i] = ring.tile([P, H], F32, name="res")
+            nc.scalar.activation(out=res[i][:], in_=summed[i][:], func=ACT.Tanh)
+            nc.sync.dma_start(out=out_dst[:, i, :], in_=res[i][:])
+
+        cast(0)
+        turn(0)
+        interleave_x(0, 0, 4, "v")
+        cast(1)
+        for s in range(TILES + LAG + 1):
+            if s + 2 < TILES:
+                cast(s + 2)
+            if s + 1 < TILES:
+                turn(s + 1)
+            a = s - LAG
+            o = s - LAG - 1
+            if 0 <= o < TILES:
+                mm2(o)
+            if 0 <= a < TILES:
+                mm1(a)
+            if s < TILES:
+                multiply(s)
+            if s == 0:
+                quantize_x(0)
+                interleave_x(1, 0, 4, "g")
+            if s == 2:
+                quantize_x(1)
+            if 0 < s <= TILES:
+                quantize_f(s - 1)
+            if 0 <= a < TILES:
+                evacuate(a)
+                quantize_a(a)
+            if 0 <= o < TILES:
+                add_bias(o)
+                finish(o)

@@ -21,7 +21,6 @@ H = 512
 G = 2
 T = 4
 TILES = 8
-LAG = 3
 FLOPS = 2 * NODES * NODES * DIN + 2 * NODES * DIN * H
 
 
@@ -29,7 +28,7 @@ def tile_controencodnet_pa_w8_kernel(tc, f_bytes, f_scale, x, w_words, w_scales,
     nc = tc.nc
     with ExitStack() as ctx:
         keep = ctx.enter_context(tc.tile_pool(name="keep", bufs=1))
-        ring = ctx.enter_context(tc.tile_pool(name="ring", bufs=4))
+        ring = ctx.enter_context(tc.tile_pool(name="ring", bufs=6))
         ps_t = ctx.enter_context(tc.psum_pool(name="ps_t", bufs=3))
         ps_a = ctx.enter_context(tc.psum_pool(name="ps_a", bufs=2))
         ps_o = ctx.enter_context(tc.psum_pool(name="ps_o", bufs=3))
@@ -141,42 +140,32 @@ def tile_controencodnet_pa_w8_kernel(tc, f_bytes, f_scale, x, w_words, w_scales,
             prod[i] = ps_o.tile([P, H], F32, name="prod")
             nc.tensor.matmul_mx(out=prod[i][:], lhsT=ac[i][:].bitcast(FP8X4), lhsT_scale=asc[i][:], rhs=wc[:].bitcast(FP8X4), rhs_scale=ws[:], start=True, stop=True)
 
+        def column_parts(i):
+            return [(0, H // 2), (H // 2, H)] if i == TILES - 1 else [(0, H)]
+
         def add_bias(i):
             summed[i] = ring.tile([P, H], F32, name="summed")
-            nc.vector.tensor_tensor(out=summed[i][:], in0=prod[i][:], in1=bias[:], op=ADD)
+            for a, b in column_parts(i):
+                nc.vector.tensor_tensor(out=summed[i][:, a:b], in0=prod[i][:, a:b], in1=bias[:, a:b], op=ADD)
 
         def finish(i):
             res[i] = ring.tile([P, H], F32, name="res")
-            nc.scalar.activation(out=res[i][:], in_=summed[i][:], func=ACT.Tanh)
-            nc.sync.dma_start(out=out_dst[:, i, :], in_=res[i][:])
+            for a, b in column_parts(i):
+                nc.scalar.activation(out=res[i][:, a:b], in_=summed[i][:, a:b], func=ACT.Tanh)
+                nc.sync.dma_start(out=out_dst[:, i, a:b], in_=res[i][:, a:b])
 
-        cast(0)
-        turn(0)
-        interleave_x(0, 0, 4, "v")
-        cast(1)
-        for s in range(TILES + LAG + 1):
-            if s + 2 < TILES:
-                cast(s + 2)
-            if s + 1 < TILES:
-                turn(s + 1)
-            a = s - LAG
-            o = s - LAG - 1
-            if 0 <= o < TILES:
-                mm2(o)
-            if 0 <= a < TILES:
-                mm1(a)
-            if s < TILES:
-                multiply(s)
+        steps = [(turn, -1), (evacuate, 5), (quantize_f, 2), (cast, -2), (multiply, 0), (mm2, 7), (quantize_a, 5), (finish, 9), (add_bias, 7), (mm1, 3)]
+        for s in range(-2, TILES + 9):
+            if s == -2:
+                interleave_x(0, 0, 4, "v")
             if s == 0:
+                interleave_x(1, 0, 2, "s")
+            if s == 1:
                 quantize_x(0)
-                interleave_x(1, 0, 4, "g")
             if s == 2:
+                interleave_x(1, 2, 4, "s")
+            if s == 3:
                 quantize_x(1)
-            if 0 < s <= TILES:
-                quantize_f(s - 1)
-            if 0 <= a < TILES:
-                evacuate(a)
-                quantize_a(a)
-            if 0 <= o < TILES:
-                add_bias(o)
-                finish(o)
+            for call, lag in steps:
+                if 0 <= s - lag < TILES:
+                    call(s - lag)

from contextlib import ExitStack

import concourse.mybir as mybir
from concourse.masks import make_identity

F32 = mybir.dt.float32
BF16 = mybir.dt.bfloat16
U32 = mybir.dt.uint32
I32 = mybir.dt.int32
U8 = mybir.dt.uint8
FP8 = mybir.dt.float8_e4m3fn
FP8X4 = mybir.dt.float8_e4m3fn_x4
MULT = mybir.AluOpType.mult
ADD = mybir.AluOpType.add
ACT = mybir.ActivationFunctionType

P = 128
NODES = 1024
DIN = 512
H = 512
G = 2
T = 4
TILES = 8
FLOPS = 2 * NODES * NODES * DIN + 2 * NODES * DIN * H


def tile_controencodnet_pa_w8_kernel(tc, f_bytes, f_scale, x, w_words, w_scales, b1, out):
    nc = tc.nc
    with ExitStack() as ctx:
        keep = ctx.enter_context(tc.tile_pool(name="keep", bufs=1))
        ring = ctx.enter_context(tc.tile_pool(name="ring", bufs=6))
        ps_t = ctx.enter_context(tc.psum_pool(name="ps_t", bufs=3))
        ps_a = ctx.enter_context(tc.psum_pool(name="ps_a", bufs=2))
        ps_o = ctx.enter_context(tc.psum_pool(name="ps_o", bufs=3))
        ctx.enter_context(tc.manual_schedule())

        bytes_src = f_bytes.rearrange("(p i) k -> p i k", i=TILES)
        out_dst = out.rearrange("(p i) h -> p i h", i=TILES)
        x_src = x.rearrange("(g p j) d -> g p j d", g=G, j=T)

        loads = [(0, 1), (1, 2), (2, 4), (4, 6), (6, 8)]
        fb = [keep.tile([P, (b - a) * NODES], U8, name="fb%d" % a, align_bytes=64) for a, b in loads]
        where = {}
        for q, (a, b) in enumerate(loads):
            for i in range(a, b):
                where[i] = (q, i - a)
        fs = keep.tile([P, G, T], F32)
        xr = [keep.tile([P, T, DIN], BF16, name="xr%d" % g, align_bytes=64) for g in range(G)]
        xg = [keep.tile([P, T * P * T], BF16, name="xg%d" % g, align_bytes=64) for g in range(G)]
        xc = [keep.tile([P, DIN], U32, name="xc%d" % g, align_bytes=64) for g in range(G)]
        xs = [keep.tile([P, DIN], U8, name="xs%d" % g, align_bytes=64) for g in range(G)]
        wc = keep.tile([P, H * T], U8, align_bytes=64)
        ws = keep.tile([P, H], U8, align_bytes=64)
        bias = keep.tile([P, H], BF16)
        ident = keep.tile([P, P], F32)
        warm = keep.tile([P, 1], F32)

        def load_f(q):
            a, b = loads[q]
            nc.sync.dma_start(out=fb[q][:].rearrange("p (i k) -> p i k", i=b - a), in_=bytes_src[:, a:b, :])

        load_f(0)
        nc.sync.dma_start(out=fs[:], in_=f_scale.rearrange("o (g p t) -> p (o g) t", g=G, t=T))
        nc.sync.dma_start(out=xr[0][:], in_=x_src[0])
        load_f(1)
        nc.sync.dma_start(out=xr[1][:], in_=x_src[1])
        load_f(2)
        nc.vector.memset(warm[:], 0.0)
        nc.scalar.activation(out=warm[:], in_=warm[:], func=ACT.Tanh)
        make_identity(nc, ident[:])
        nc.gpsimd.memset(ws[:].bitcast(U32), 0)
        load_f(3)
        nc.sync.dma_start(out=wc[:], in_=w_words[0].rearrange("p n t -> p (n t)"))
        for q in range(4):
            nc.sync.dma_start(out=ws[32 * q : 32 * q + 4, :].bitcast(I32), in_=w_scales[0, 4 * q : 4 * q + 4, :].bitcast(I32))
        load_f(4)
        nc.sync.dma_start(out=bias[:], in_=b1.partition_broadcast(P))

        wide, turned, fg, fc, fsc = {}, {}, {}, {}, {}
        agg, ag, ac, asc, prod, summed, res = {}, {}, {}, {}, {}, {}, {}

        def cast(i):
            q, k = where[i]
            wide[i] = ring.tile([P, NODES], BF16, name="wide", align_bytes=64)
            nc.scalar.copy(out=wide[i][:], in_=fb[q][:, k * NODES : (k + 1) * NODES].bitcast(FP8))

        def turn(i):
            turned[i] = ps_t.tile([P, 2, G, P], F32, name="turned")
            words = wide[i][:].bitcast(F32)
            for g in range(G):
                for u in range(2):
                    nc.tensor.transpose(turned[i][:, u, g, :], words[:, 256 * g + u : 256 * (g + 1) : 2], ident[:])

        def multiply(i):
            fg[i] = ring.tile([P, G, P * T], BF16, name="fg", align_bytes=64)
            nc.vector.tensor_tensor(
                out=fg[i][:].rearrange("p g (n u e) -> p g n u e", u=2, e=2),
                in0=turned[i][:].rearrange("p u g n -> p (u g n)").bitcast(BF16).rearrange("p (u g n e) -> p g n u e", u=2, g=G, e=2),
                in1=fs[:].unsqueeze(2).to_broadcast([P, G, P, T]).rearrange("p g n (u e) -> p g n u e", u=2),
                op=MULT,
            )

        def quantize_f(i):
            fc[i] = ring.tile([P, G * P], U32, name="fc", align_bytes=64)
            fsc[i] = ring.tile([P, G * P], U8, name="fsc", align_bytes=64)
            nc.vector.quantize_mx(out=fc[i][:].bitcast(FP8X4), scales=fsc[i][:], in_=fg[i][:].rearrange("p g n -> p (g n)"))

        def interleave_x(g, t0, t1, engine):
            dst = xg[g][:].rearrange("p (t m j) -> p t m j", t=T, j=T)[:, t0:t1]
            src = xr[g][:].rearrange("p j (m t) -> p t m j", t=T)[:, t0:t1]
            if engine == "v":
                nc.vector.tensor_copy(out=dst, in_=src)
            elif engine == "s":
                nc.scalar.copy(out=dst, in_=src)
            else:
                nc.gpsimd.tensor_scalar(out=dst, in0=src, scalar1=1.0, scalar2=0.0, op0=MULT, op1=ADD)

        def quantize_x(g):
            nc.vector.quantize_mx(out=xc[g][:].bitcast(FP8X4), scales=xs[g][:], in_=xg[g][:])

        def mm1(i):
            agg[i] = ps_a.tile([P, T, P], F32, name="agg")
            for t in range(T):
                cols = slice(P * t, P * (t + 1))
                for g in range(G):
                    rows = slice(P * g, P * (g + 1))
                    nc.tensor.matmul_mx(out=agg[i][:, t, :], lhsT=xc[g][:, cols].bitcast(FP8X4), lhsT_scale=xs[g][:, cols],
                                        rhs=fc[i][:, rows].bitcast(FP8X4), rhs_scale=fsc[i][:, rows], start=(g == 0), stop=(g == G - 1))

        def evacuate(i):
            ag[i] = ring.tile([P, P * T], BF16, name="ag", align_bytes=64)
            nc.scalar.copy(out=ag[i][:].rearrange("p (n t) -> p n t", t=T), in_=agg[i][:].rearrange("p t n -> p n t"))

        def quantize_a(i):
            ac[i] = ring.tile([P, P], U32, name="ac", align_bytes=64)
            asc[i] = ring.tile([P, P], U8, name="asc", align_bytes=64)
            nc.vector.quantize_mx(out=ac[i][:].bitcast(FP8X4), scales=asc[i][:], in_=ag[i][:])

        def mm2(i):
            prod[i] = ps_o.tile([P, H], F32, name="prod")
            nc.tensor.matmul_mx(out=prod[i][:], lhsT=ac[i][:].bitcast(FP8X4), lhsT_scale=asc[i][:], rhs=wc[:].bitcast(FP8X4), rhs_scale=ws[:], start=True, stop=True)

        def column_parts(i):
            return [(0, H // 2), (H // 2, H)] if i == TILES - 1 else [(0, H)]

        def add_bias(i):
            summed[i] = ring.tile([P, H], F32, name="summed")
            for a, b in column_parts(i):
                nc.vector.tensor_tensor(out=summed[i][:, a:b], in0=prod[i][:, a:b], in1=bias[:, a:b], op=ADD)

        def finish(i):
            res[i] = ring.tile([P, H], F32, name="res")
            for a, b in column_parts(i):
                nc.scalar.activation(out=res[i][:, a:b], in_=summed[i][:, a:b], func=ACT.Tanh)
                nc.sync.dma_start(out=out_dst[:, i, a:b], in_=res[i][:, a:b])

        steps = [(turn, -1), (evacuate, 5), (quantize_f, 2), (cast, -2), (multiply, 0), (mm2, 7), (quantize_a, 5), (finish, 9), (add_bias, 7), (mm1, 3)]
        for s in range(-2, TILES + 9):
            if s == -2:
                interleave_x(0, 0, 4, "v")
            if s == 0:
                interleave_x(1, 0, 2, "s")
            if s == 1:
                quantize_x(0)
            if s == 2:
                interleave_x(1, 2, 4, "s")
            if s == 3:
                quantize_x(1)
            for call, lag in steps:
                if 0 <= s - lag < TILES:
                    call(s - lag)
